import numpy as np
import ml_dtypes


def mxq(x, axis, fmt="e4m3"):
    dtype, down = {"e4m3": (ml_dtypes.float8_e4m3fn, 7), "e5m2": (ml_dtypes.float8_e5m2, 14)}[fmt]
    v = np.moveaxis(np.asarray(x, np.float32).astype(ml_dtypes.bfloat16).astype(np.float64), axis, -1)
    blocks = v.reshape(v.shape[:-1] + (-1, 32))
    amax = np.abs(blocks).max(-1, keepdims=True)
    byte = np.maximum(np.where(amax > 0, np.frexp(amax)[1] - 1 + 127, 0) - down, 1)
    scale = np.exp2(byte - 127.0)
    codes = (blocks / scale).astype(np.float32).astype(dtype).astype(np.float64)
    return np.moveaxis((codes * scale).reshape(v.shape), -1, axis)


WIDE = False


def mx_kscale(k):
    if not WIDE:
        return np.ones(k)
    levels = np.array([10, -10, 5, -5, 0])
    a = np.random.permutation(np.resize(levels, k // 512 * 4)).reshape(k // 512, 4)
    idx = np.arange(k)
    return np.exp2(a[idx // 512, idx % 128 // 32])


BF16 = ml_dtypes.bfloat16


def bf(x):
    return np.asarray(x, np.float32).astype(BF16)


def f64(x):
    return np.asarray(x).astype(np.float64)


B, S, D, H, DK, DV, C = 1, 1024, 1024, 16, 128, 128, 512


def setup_inputs():
    t = mx_kscale(S)
    return {"q_rot": bf(np.random.standard_normal((B, H, S, DK)) * 0.3),
            "k_rot": bf(np.random.standard_normal((B, H, S, DK)) * 0.3 * t[:, None]),
            "v": bf(np.random.standard_normal((B, H, S, DV)) * 0.5 / t[:, None])}


def reference(q_rot, k_rot, v):
    q, k = f64(q_rot), f64(k_rot)
    vq = mxq(f64(v), 2, "e4m3")
    gamma = 1.0 - 2.0 ** (-5.0 - np.arange(H, dtype=np.float64))
    pos = np.arange(S, dtype=np.float64)
    blocks = []
    for r in range(0, S, C):
        n = r + C
        pm = pos[r:n, None] - pos[None, :n]
        decay = np.where(pm >= 0, gamma[:, None, None] ** np.maximum(pm, 0.0), 0.0)
        scores = (q[:, :, r:n] @ k[:, :, :n].transpose(0, 1, 3, 2)) * decay
        blocks.append(mxq(scores, 3, "e4m3") @ vq[:, :, :n])
    return np.concatenate(blocks, axis=2)

@@ -1,0 +1,193 @@
+import math
+from contextlib import ExitStack
+
+import concourse.mybir as mybir
+from concourse.masks import make_identity
+
+BF16 = mybir.dt.bfloat16
+F32 = mybir.dt.float32
+I32 = mybir.dt.int32
+U32 = mybir.dt.uint32
+U8 = mybir.dt.uint8
+FP8X4 = mybir.dt.float8_e4m3fn_x4
+
+HEADS = 16
+SEQ = 1024
+FEAT = 128
+P = 128
+PACK = 4
+TILES = SEQ // P
+PASSES = SEQ // (P * PACK)
+
+ROUNDS = ((0, 0), (0, 4), (1, 4))
+
+MASKED = 2.0**30
+
+LOAD_AHEAD = 3
+
+FLOPS = 2 * 2 * HEADS * FEAT * (512 * 512 + 512 * 1024)
+
+
+def tile_gatedmultiscaleretentionlayer_pb_kernel(tc, q_rot, k_rot, v, out):
+    nc = tc.nc
+    q_rows = q_rot.rearrange("b h (n p) d -> p (b h n) d", p=P)
+    k_rows = k_rot.rearrange("b h (n p) d -> p (b h n) d", p=P)
+    v_rows = v.rearrange("b h (n p) d -> p (b h n) d", p=P)
+    out_rows = out.rearrange("b h (n p) d -> p (b h n) d", p=P)
+
+    with ExitStack() as ctx:
+        fixed = ctx.enter_context(tc.tile_pool(name="fixed", bufs=1))
+        loads = ctx.enter_context(tc.tile_pool(name="loads", bufs=LOAD_AHEAD + 1))
+        per_head = ctx.enter_context(tc.tile_pool(name="per_head", bufs=2))
+        v_mx = ctx.enter_context(tc.tile_pool(name="v_mx", bufs=3))
+        stores = ctx.enter_context(tc.tile_pool(name="stores", bufs=4))
+        transpose_psum = ctx.enter_context(tc.psum_pool(name="transpose_psum", bufs=1))
+        score_psum = ctx.enter_context(tc.psum_pool(name="score_psum", bufs=4))
+        out_psum = ctx.enter_context(tc.psum_pool(name="out_psum", bufs=2))
+
+        identity = fixed.tile([P, P], BF16)
+        make_identity(nc, identity[:])
+
+        exponent_int = fixed.tile([P, TILES, P], I32)
+        nc.gpsimd.iota(
+            exponent_int[:], pattern=[[-P, TILES], [1, P]], base=P * (TILES - 1), channel_multiplier=-1
+        )
+        exponent = fixed.tile([P, TILES, P], F32)
+        nc.vector.tensor_copy(out=exponent[:], in_=exponent_int[:])
+        nc.gpsimd.affine_select(
+            out=exponent[:, TILES - 1, :],
+            in_=exponent[:, TILES - 1, :],
+            pattern=[[1, P]],
+            compare_op=mybir.AluOpType.is_ge,
+            fill=MASKED,
+            base=0,
+            channel_multiplier=-1,
+        )
+
+        grouped = []
+        codes = []
+        scales = []
+        for r in range(len(ROUNDS)):
+            grouped.append(fixed.tile([P, PACK, P, PACK], BF16, name="grouped%d" % r, align_bytes=64))
+            codes.append(fixed.tile([P, PACK, P], U32, name="codes%d" % r, align_bytes=64))
+            scales.append(fixed.tile([P, PACK, P], U8, name="scales%d" % r, align_bytes=64))
+        nc.vector.memset(grouped[0][:], 0.0)
+        nc.vector.memset(grouped[2][:], 0.0)
+
+        raw = {}
+        ready = {}
+
+        def load(h):
+            rows = slice(TILES * h, TILES * (h + 1))
+            k_sb = loads.tile([P, TILES, FEAT], BF16, tag="k_sb")
+            nc.sync.dma_start(out=k_sb[:], in_=k_rows[:, rows, :])
+            q_sb = loads.tile([P, TILES, FEAT], BF16, tag="q_sb")
+            nc.sync.dma_start(out=q_sb[:], in_=q_rows[:, rows, :])
+            v_sb = loads.tile([P, TILES, FEAT], BF16, tag="v_sb")
+            nc.sync.dma_start(out=v_sb[:], in_=v_rows[:, rows, :])
+            raw[h] = (q_sb, k_sb, v_sb)
+
+        def transposed(rows_sb, tag):
+            bank = transpose_psum.tile([P, TILES, P], BF16, tag=tag + "_psum")
+            for n in range(TILES):
+                nc.tensor.transpose(bank[:, n, :], rows_sb[:, n, :], identity[:])
+            result = per_head.tile([P, TILES, P], BF16, tag=tag)
+            nc.scalar.copy(out=result[:], in_=bank[:])
+            return result
+
+        def prepare(h):
+            q_sb, k_sb, v_sb = raw.pop(h)
+            kT = transposed(k_sb, "kT")
+            qT = transposed(q_sb, "qT")
+
+            gamma = 1.0 - 2.0 ** (-5 - h)
+            decay = per_head.tile([P, TILES, P], F32, tag="decay")
+            nc.scalar.activation(
+                out=decay[:], in_=exponent[:], func=mybir.ActivationFunctionType.Exp, scale=math.log(gamma)
+            )
+
+            v_grouped = per_head.tile([P, PASSES, FEAT, PACK], BF16, tag="v_grouped", align_bytes=64)
+            nc.scalar.copy(out=v_grouped[:], in_=v_sb[:].rearrange("p (g t) d -> p g d t", t=PACK))
+            v_codes = v_mx.tile([P, PASSES, FEAT], U32, tag="v_codes", align_bytes=64)
+            v_scales = v_mx.tile([P, PASSES, FEAT], U8, tag="v_scales", align_bytes=64)
+            nc.vector.quantize_mx(
+                out=v_codes[:].rearrange("p g d -> p (g d)").bitcast(FP8X4),
+                scales=v_scales[:].rearrange("p g d -> p (g d)"),
+                in_=v_grouped[:].rearrange("p g d t -> p (g d t)"),
+            )
+            ready[h] = (qT, kT, decay, v_codes, v_scales)
+
+        def decayed_scores(h, r):
+            qT, kT, decay = ready[h][0:3]
+            g, first_query_tile = ROUNDS[r]
+            for c in range(PACK):
+                query_tile = first_query_tile + c
+                behind = query_tile - PACK * g
+                planes = min(behind + 1, PACK)
+                bank = score_psum.tile([P, PACK, P], F32, tag="scores")
+                for t in range(planes):
+                    nc.tensor.matmul(
+                        out=bank[:, t, :],
+                        lhsT=kT[:, PACK * g + t, :],
+                        rhs=qT[:, query_tile, :],
+                        start=True,
+                        stop=True,
+                    )
+                first_plane = TILES - 1 - behind
+                nc.vector.tensor_tensor(
+                    out=grouped[r][:, c, :, 0:planes],
+                    in0=bank[:, 0:planes, :].rearrange("p t i -> p i t"),
+                    in1=decay[:, first_plane : first_plane + planes, :].rearrange("p t i -> p i t"),
+                    op=mybir.AluOpType.mult,
+                )
+
+        def quantise_scores(r):
+            nc.vector.quantize_mx(
+                out=codes[r][:].rearrange("p c i -> p (c i)").bitcast(FP8X4),
+                scales=scales[r][:].rearrange("p c i -> p (c i)"),
+                in_=grouped[r][:].rearrange("p c i t -> p (c i t)"),
+            )
+
+        def retention(h, rounds_of_half, half):
+            v_codes, v_scales = ready[h][3:5]
+            bank = out_psum.tile([P, PACK, FEAT], F32, tag="out")
+            for c in range(PACK):
+                for r in rounds_of_half:
+                    g = ROUNDS[r][0]
+                    nc.tensor.matmul_mx(
+                        out=bank[:, c, :],
+                        lhsT=codes[r][:, c, :].bitcast(FP8X4),
+                        lhsT_scale=scales[r][:, c, :],
+                        rhs=v_codes[:, g, :].bitcast(FP8X4),
+                        rhs_scale=v_scales[:, g, :],
+                        start=(r == rounds_of_half[0]),
+                        stop=(r == rounds_of_half[-1]),
+                    )
+            result = stores.tile([P, PACK, FEAT], F32, tag="result")
+            nc.scalar.copy(out=result[:], in_=bank[:])
+            first = TILES * h + PACK * half
+            nc.sync.dma_start(out=out_rows[:, first : first + PACK, :], in_=result[:])
+
+        def finish(h, r):
+            quantise_scores(r)
+            if r == 0:
+                retention(h, (0,), 0)
+            if r == 2:
+                retention(h, (1, 2), 1)
+                ready.pop(h)
+
+        for h in range(LOAD_AHEAD):
+            load(h)
+        prepare(0)
+        waiting = []
+        for h in range(HEADS):
+            if h + LOAD_AHEAD < HEADS:
+                load(h + LOAD_AHEAD)
+            if h + 1 < HEADS:
+                prepare(h + 1)
+            for r in range(len(ROUNDS)):
+                decayed_scores(h, r)
+                if waiting:
+                    finish(*waiting.pop())
+                waiting.append((h, r))
+        finish(*waiting.pop())

@@ -10,6 +10,7 @@ I32 = mybir.dt.int32
 U32 = mybir.dt.uint32
 U8 = mybir.dt.uint8
 FP8X4 = mybir.dt.float8_e4m3fn_x4
+MULT = mybir.AluOpType.mult
 
 HEADS = 16
 SEQ = 1024
@@ -21,7 +22,7 @@ PASSES = SEQ // (P * PACK)
 
 ROUNDS = ((0, 0), (0, 4), (1, 4))
 
-MASKED = 2.0**30
+TABLE_PLANES = PACK + 1
 
 LOAD_AHEAD = 3
 
@@ -48,20 +49,18 @@ def tile_gatedmultiscaleretentionlayer_pb_kernel(tc, q_rot, k_rot, v, out):
         identity = fixed.tile([P, P], BF16)
         make_identity(nc, identity[:])
 
-        exponent_int = fixed.tile([P, TILES, P], I32)
+        distance = fixed.tile([P, P, TABLE_PLANES], I32)
         nc.gpsimd.iota(
-            exponent_int[:], pattern=[[-P, TILES], [1, P]], base=P * (TILES - 1), channel_multiplier=-1
+            distance[:], pattern=[[1, P], [-P, TABLE_PLANES]], base=P * PACK, channel_multiplier=-1
         )
-        exponent = fixed.tile([P, TILES, P], F32)
-        nc.vector.tensor_copy(out=exponent[:], in_=exponent_int[:])
-        nc.gpsimd.affine_select(
-            out=exponent[:, TILES - 1, :],
-            in_=exponent[:, TILES - 1, :],
-            pattern=[[1, P]],
-            compare_op=mybir.AluOpType.is_ge,
-            fill=MASKED,
-            base=0,
-            channel_multiplier=-1,
+        exponent = fixed.tile([P, P, TABLE_PLANES], F32)
+        nc.vector.scalar_tensor_tensor(
+            out=exponent[:],
+            in0=distance[:],
+            scalar=-(2.0**30),
+            in1=distance[:],
+            op0=MULT,
+            op1=mybir.AluOpType.max,
         )
 
         grouped = []
@@ -100,10 +99,12 @@ def tile_gatedmultiscaleretentionlayer_pb_kernel(tc, q_rot, k_rot, v, out):
             kT = transposed(k_sb, "kT")
             qT = transposed(q_sb, "qT")
 
-            gamma = 1.0 - 2.0 ** (-5 - h)
-            decay = per_head.tile([P, TILES, P], F32, tag="decay")
+            decay = per_head.tile([P, P, TABLE_PLANES], F32, tag="decay")
             nc.scalar.activation(
-                out=decay[:], in_=exponent[:], func=mybir.ActivationFunctionType.Exp, scale=math.log(gamma)
+                out=decay[:],
+                in_=exponent[:],
+                func=mybir.ActivationFunctionType.Exp,
+                scale=math.log(1.0 - 2.0 ** (-5 - h)),
             )
 
             v_grouped = per_head.tile([P, PASSES, FEAT, PACK], BF16, tag="v_grouped", align_bytes=64)
@@ -119,27 +120,37 @@ def tile_gatedmultiscaleretentionlayer_pb_kernel(tc, q_rot, k_rot, v, out):
 
         def decayed_scores(h, r):
             qT, kT, decay = ready[h][0:3]
+            gamma = 1.0 - 2.0 ** (-5 - h)
             g, first_query_tile = ROUNDS[r]
             for c in range(PACK):
                 query_tile = first_query_tile + c
                 behind = query_tile - PACK * g
                 planes = min(behind + 1, PACK)
-                bank = score_psum.tile([P, PACK, P], F32, tag="scores")
+                bank = score_psum.tile([P, P, PACK], F32, tag="scores")
                 for t in range(planes):
                     nc.tensor.matmul(
-                        out=bank[:, t, :],
+                        out=bank[:, :, t],
                         lhsT=kT[:, PACK * g + t, :],
                         rhs=qT[:, query_tile, :],
                         start=True,
                         stop=True,
                     )
-                first_plane = TILES - 1 - behind
-                nc.vector.tensor_tensor(
-                    out=grouped[r][:, c, :, 0:planes],
-                    in0=bank[:, 0:planes, :].rearrange("p t i -> p i t"),
-                    in1=decay[:, first_plane : first_plane + planes, :].rearrange("p t i -> p i t"),
-                    op=mybir.AluOpType.mult,
-                )
+                if behind < PACK:
+                    nc.vector.tensor_tensor(
+                        out=grouped[r][:, c, :, 0:planes],
+                        in0=bank[:, :, 0:planes],
+                        in1=decay[:, :, PACK - behind : TABLE_PLANES],
+                        op=MULT,
+                    )
+                else:
+                    nc.vector.scalar_tensor_tensor(
+                        out=grouped[r][:, c, :, :],
+                        in0=bank[:],
+                        scalar=gamma ** (P * (behind - PACK)),
+                        in1=decay[:, :, 0:PACK],
+                        op0=MULT,
+                        op1=MULT,
+                    )
 
         def quantise_scores(r):
             nc.vector.quantize_mx(

@@ -24,9 +24,26 @@ ROUNDS = ((0, 0), (0, 4), (1, 4))
 
 TABLE_PLANES = PACK + 1
 
+GPSIMD_MAX_PLANES = 2
+GPSIMD_FULL_BANKS = 1
+
 LOAD_AHEAD = 3
+SCORE_BANKS = 5
 
 FLOPS = 2 * 2 * HEADS * FEAT * (512 * 512 + 512 * 1024)
+
+
+def tiles_behind(r, c):
+    g, first_query_tile = ROUNDS[r]
+    return first_query_tile + c - PACK * g
+
+
+def planes_of(r, c):
+    return min(tiles_behind(r, c) + 1, PACK)
+
+
+def on_gpsimd(r, c):
+    return planes_of(r, c) <= GPSIMD_MAX_PLANES or (r == 1 and c < GPSIMD_FULL_BANKS)
 
 
 def tile_gatedmultiscaleretentionlayer_pb_kernel(tc, q_rot, k_rot, v, out):
@@ -37,14 +54,32 @@ def tile_gatedmultiscaleretentionlayer_pb_kernel(tc, q_rot, k_rot, v, out):
     out_rows = out.rearrange("b h (n p) d -> p (b h n) d", p=P)
 
     with ExitStack() as ctx:
+        ctx.enter_context(tc.manual_schedule())
         fixed = ctx.enter_context(tc.tile_pool(name="fixed", bufs=1))
         loads = ctx.enter_context(tc.tile_pool(name="loads", bufs=LOAD_AHEAD + 1))
         per_head = ctx.enter_context(tc.tile_pool(name="per_head", bufs=2))
         v_mx = ctx.enter_context(tc.tile_pool(name="v_mx", bufs=3))
+        staging = ctx.enter_context(tc.tile_pool(name="staging", bufs=3))
         stores = ctx.enter_context(tc.tile_pool(name="stores", bufs=4))
         transpose_psum = ctx.enter_context(tc.psum_pool(name="transpose_psum", bufs=1))
-        score_psum = ctx.enter_context(tc.psum_pool(name="score_psum", bufs=4))
+        score_psum = ctx.enter_context(tc.psum_pool(name="score_psum", bufs=SCORE_BANKS))
         out_psum = ctx.enter_context(tc.psum_pool(name="out_psum", bufs=2))
+
+        q_sb, k_sb, v_sb = {}, {}, {}
+        qT, kT, decay = {}, {}, {}
+        v_grouped, v_codes, v_scales = {}, {}, {}
+
+        def load(h):
+            rows = slice(TILES * h, TILES * (h + 1))
+            k_sb[h] = loads.tile([P, TILES, FEAT], BF16, name="k_sb", tag="k_sb")
+            nc.sync.dma_start(out=k_sb[h][:], in_=k_rows[:, rows, :])
+            q_sb[h] = loads.tile([P, TILES, FEAT], BF16, name="q_sb", tag="q_sb")
+            nc.sync.dma_start(out=q_sb[h][:], in_=q_rows[:, rows, :])
+            v_sb[h] = loads.tile([P, TILES, FEAT], BF16, name="v_sb", tag="v_sb")
+            nc.sync.dma_start(out=v_sb[h][:], in_=v_rows[:, rows, :])
+
+        for h in range(LOAD_AHEAD):
+            load(h)
 
         identity = fixed.tile([P, P], BF16)
         make_identity(nc, identity[:])
@@ -73,84 +108,82 @@ def tile_gatedmultiscaleretentionlayer_pb_kernel(tc, q_rot, k_rot, v, out):
         nc.vector.memset(grouped[0][:], 0.0)
         nc.vector.memset(grouped[2][:], 0.0)
 
-        raw = {}
-        ready = {}
-
-        def load(h):
-            rows = slice(TILES * h, TILES * (h + 1))
-            k_sb = loads.tile([P, TILES, FEAT], BF16, tag="k_sb")
-            nc.sync.dma_start(out=k_sb[:], in_=k_rows[:, rows, :])
-            q_sb = loads.tile([P, TILES, FEAT], BF16, tag="q_sb")
-            nc.sync.dma_start(out=q_sb[:], in_=q_rows[:, rows, :])
-            v_sb = loads.tile([P, TILES, FEAT], BF16, tag="v_sb")
-            nc.sync.dma_start(out=v_sb[:], in_=v_rows[:, rows, :])
-            raw[h] = (q_sb, k_sb, v_sb)
-
         def transposed(rows_sb, tag):
-            bank = transpose_psum.tile([P, TILES, P], BF16, tag=tag + "_psum")
+            bank = transpose_psum.tile([P, TILES, P], BF16, tag="transposes")
             for n in range(TILES):
                 nc.tensor.transpose(bank[:, n, :], rows_sb[:, n, :], identity[:])
             result = per_head.tile([P, TILES, P], BF16, tag=tag)
             nc.scalar.copy(out=result[:], in_=bank[:])
             return result
 
-        def prepare(h):
-            q_sb, k_sb, v_sb = raw.pop(h)
-            kT = transposed(k_sb, "kT")
-            qT = transposed(q_sb, "qT")
+        def prepare(h, part):
+            if part == 0:
+                kT[h] = transposed(k_sb.pop(h), "kT")
+                decay[h] = per_head.tile([P, P, TABLE_PLANES], F32, name="decay", tag="decay")
+                nc.scalar.activation(
+                    out=decay[h][:],
+                    in_=exponent[:],
+                    func=mybir.ActivationFunctionType.Exp,
+                    scale=math.log(1.0 - 2.0 ** (-5 - h)),
+                )
+            if part == 1:
+                qT[h] = transposed(q_sb.pop(h), "qT")
+            if part == 2:
+                v_grouped[h] = per_head.tile(
+                    [P, PASSES, FEAT, PACK], BF16, name="v_grouped", tag="v_grouped", align_bytes=64
+                )
+                nc.scalar.copy(
+                    out=v_grouped[h][:], in_=v_sb.pop(h)[:].rearrange("p (g t) d -> p g d t", t=PACK)
+                )
 
-            decay = per_head.tile([P, P, TABLE_PLANES], F32, tag="decay")
-            nc.scalar.activation(
-                out=decay[:],
-                in_=exponent[:],
-                func=mybir.ActivationFunctionType.Exp,
-                scale=math.log(1.0 - 2.0 ** (-5 - h)),
-            )
-
-            v_grouped = per_head.tile([P, PASSES, FEAT, PACK], BF16, tag="v_grouped", align_bytes=64)
-            nc.scalar.copy(out=v_grouped[:], in_=v_sb[:].rearrange("p (g t) d -> p g d t", t=PACK))
-            v_codes = v_mx.tile([P, PASSES, FEAT], U32, tag="v_codes", align_bytes=64)
-            v_scales = v_mx.tile([P, PASSES, FEAT], U8, tag="v_scales", align_bytes=64)
+        def quantise_v(h):
+            v_codes[h] = v_mx.tile([P, PASSES, FEAT], U32, name="v_codes", tag="v_codes", align_bytes=64)
+            v_scales[h] = v_mx.tile([P, PASSES, FEAT], U8, name="v_scales", tag="v_scales", align_bytes=64)
             nc.vector.quantize_mx(
-                out=v_codes[:].rearrange("p g d -> p (g d)").bitcast(FP8X4),
-                scales=v_scales[:].rearrange("p g d -> p (g d)"),
-                in_=v_grouped[:].rearrange("p g d t -> p (g d t)"),
+                out=v_codes[h][:].rearrange("p g d -> p (g d)").bitcast(FP8X4),
+                scales=v_scales[h][:].rearrange("p g d -> p (g d)"),
+                in_=v_grouped.pop(h)[:].rearrange("p g d t -> p (g d t)"),
             )
-            ready[h] = (qT, kT, decay, v_codes, v_scales)
 
-        def decayed_scores(h, r):
-            qT, kT, decay = ready[h][0:3]
-            gamma = 1.0 - 2.0 ** (-5 - h)
+        def score_matmuls(h, r, c):
             g, first_query_tile = ROUNDS[r]
-            for c in range(PACK):
-                query_tile = first_query_tile + c
-                behind = query_tile - PACK * g
-                planes = min(behind + 1, PACK)
-                bank = score_psum.tile([P, P, PACK], F32, tag="scores")
-                for t in range(planes):
-                    nc.tensor.matmul(
-                        out=bank[:, :, t],
-                        lhsT=kT[:, PACK * g + t, :],
-                        rhs=qT[:, query_tile, :],
-                        start=True,
-                        stop=True,
-                    )
-                if behind < PACK:
-                    nc.vector.tensor_tensor(
-                        out=grouped[r][:, c, :, 0:planes],
-                        in0=bank[:, :, 0:planes],
-                        in1=decay[:, :, PACK - behind : TABLE_PLANES],
-                        op=MULT,
-                    )
-                else:
-                    nc.vector.scalar_tensor_tensor(
-                        out=grouped[r][:, c, :, :],
-                        in0=bank[:],
-                        scalar=gamma ** (P * (behind - PACK)),
-                        in1=decay[:, :, 0:PACK],
-                        op0=MULT,
-                        op1=MULT,
-                    )
+            bank = score_psum.tile([P, P, PACK], F32, tag="scores")
+            for t in range(planes_of(r, c)):
+                nc.tensor.matmul(
+                    out=bank[:, :, t],
+                    lhsT=kT[h][:, PACK * g + t, :],
+                    rhs=qT[h][:, first_query_tile + c, :],
+                    start=True,
+                    stop=True,
+                )
+            return bank
+
+        def decay_of(h, r, c):
+            behind = tiles_behind(r, c)
+            if behind < PACK:
+                return 1.0, decay[h][:, :, PACK - behind : TABLE_PLANES]
+            gamma = 1.0 - 2.0 ** (-5 - h)
+            return gamma ** (P * (behind - PACK)), decay[h][:, :, 0:PACK]
+
+        def decay_on_vector(h, r, c, bank):
+            planes = planes_of(r, c)
+            factor, table = decay_of(h, r, c)
+            nc.vector.scalar_tensor_tensor(
+                out=grouped[r][:, c, :, 0:planes],
+                in0=bank[:, :, 0:planes],
+                scalar=factor,
+                in1=table,
+                op0=MULT,
+                op1=MULT,
+            )
+
+        def decay_on_gpsimd(h, r, c, bank):
+            planes = planes_of(r, c)
+            factor, table = decay_of(h, r, c)
+            staged = staging.tile([P, P * PACK], F32, tag="staged")
+            packed = staged[:, 0 : P * planes].rearrange("p (i t) -> p i t", t=planes)
+            nc.scalar.mul(out=packed, in_=bank[:, :, 0:planes], mul=factor)
+            nc.gpsimd.tensor_tensor(out=grouped[r][:, c, :, 0:planes], in0=packed, in1=table, op=MULT)
 
         def quantise_scores(r):
             nc.vector.quantize_mx(
@@ -159,8 +192,8 @@ def tile_gatedmultiscaleretentionlayer_pb_kernel(tc, q_rot, k_rot, v, out):
                 in_=grouped[r][:].rearrange("p c i t -> p (c i t)"),
             )
 
-        def retention(h, rounds_of_half, half):
-            v_codes, v_scales = ready[h][3:5]
+        def retention(h, half):
+            rounds_of_half = ((0,), (1, 2))[half]
             bank = out_psum.tile([P, PACK, FEAT], F32, tag="out")
             for c in range(PACK):
                 for r in rounds_of_half:
@@ -169,8 +202,8 @@ def tile_gatedmultiscaleretentionlayer_pb_kernel(tc, q_rot, k_rot, v, out):
                         out=bank[:, c, :],
                         lhsT=codes[r][:, c, :].bitcast(FP8X4),
                         lhsT_scale=scales[r][:, c, :],
-                        rhs=v_codes[:, g, :].bitcast(FP8X4),
-                        rhs_scale=v_scales[:, g, :],
+                        rhs=v_codes[h][:, g, :].bitcast(FP8X4),
+                        rhs_scale=v_scales[h][:, g, :],
                         start=(r == rounds_of_half[0]),
                         stop=(r == rounds_of_half[-1]),
                     )
@@ -179,26 +212,34 @@ def tile_gatedmultiscaleretentionlayer_pb_kernel(tc, q_rot, k_rot, v, out):
             first = TILES * h + PACK * half
             nc.sync.dma_start(out=out_rows[:, first : first + PACK, :], in_=result[:])
 
-        def finish(h, r):
-            quantise_scores(r)
+        def retention_after(h, r):
             if r == 0:
-                retention(h, (0,), 0)
+                retention(h, 0)
             if r == 2:
-                retention(h, (1, 2), 1)
-                ready.pop(h)
+                retention(h, 1)
 
-        for h in range(LOAD_AHEAD):
-            load(h)
-        prepare(0)
-        waiting = []
-        for h in range(HEADS):
-            if h + LOAD_AHEAD < HEADS:
+        for part in range(3):
+            prepare(0, part)
+
+        steps = [(h, r) for h in range(HEADS) for r in range(len(ROUNDS))]
+        for s, (h, r) in enumerate(steps):
+            if r == 0 and h + LOAD_AHEAD < HEADS:
                 load(h + LOAD_AHEAD)
+            banks = [score_matmuls(h, r, c) for c in range(PACK)]
+            for c in range(PACK):
+                if on_gpsimd(r, c):
+                    decay_on_gpsimd(h, r, c, banks[c])
             if h + 1 < HEADS:
-                prepare(h + 1)
-            for r in range(len(ROUNDS)):
-                decayed_scores(h, r)
-                if waiting:
-                    finish(*waiting.pop())
-                waiting.append((h, r))
-        finish(*waiting.pop())
+                prepare(h + 1, r)
+            if s >= 2:
+                retention_after(*steps[s - 2])
+            for c in range(PACK):
+                if not on_gpsimd(r, c):
+                    decay_on_vector(h, r, c, banks[c])
+            if s >= 1:
+                quantise_scores(steps[s - 1][1])
+            if r == 0:
+                quantise_v(h)
+        retention_after(*steps[-2])
+        quantise_scores(steps[-1][1])
+        retention_after(*steps[-1])

@@ -28,7 +28,7 @@ GPSIMD_MAX_PLANES = 2
 GPSIMD_FULL_BANKS = 1
 
 LOAD_AHEAD = 3
-SCORE_BANKS = 5
+SCORE_BANKS = 4
 
 FLOPS = 2 * 2 * HEADS * FEAT * (512 * 512 + 512 * 1024)
 
@@ -46,6 +46,12 @@ def on_gpsimd(r, c):
     return planes_of(r, c) <= GPSIMD_MAX_PLANES or (r == 1 and c < GPSIMD_FULL_BANKS)
 
 
+ALL_BANKS = [(r, c) for r in range(len(ROUNDS)) for c in range(PACK)]
+GPSIMD_BANKS = [rc for rc in ALL_BANKS if on_gpsimd(*rc)]
+VECTOR_BANKS = [rc for rc in ALL_BANKS if not on_gpsimd(*rc)]
+BANKS = GPSIMD_BANKS + VECTOR_BANKS
+
+
 def tile_gatedmultiscaleretentionlayer_pb_kernel(tc, q_rot, k_rot, v, out):
     nc = tc.nc
     q_rows = q_rot.rearrange("b h (n p) d -> p (b h n) d", p=P)
@@ -58,14 +64,14 @@ def tile_gatedmultiscaleretentionlayer_pb_kernel(tc, q_rot, k_rot, v, out):
         fixed = ctx.enter_context(tc.tile_pool(name="fixed", bufs=1))
         loads = ctx.enter_context(tc.tile_pool(name="loads", bufs=LOAD_AHEAD + 1))
         per_head = ctx.enter_context(tc.tile_pool(name="per_head", bufs=2))
-        v_mx = ctx.enter_context(tc.tile_pool(name="v_mx", bufs=3))
-        staging = ctx.enter_context(tc.tile_pool(name="staging", bufs=3))
+        staging = ctx.enter_context(tc.tile_pool(name="staging", bufs=len(GPSIMD_BANKS)))
         stores = ctx.enter_context(tc.tile_pool(name="stores", bufs=4))
-        transpose_psum = ctx.enter_context(tc.psum_pool(name="transpose_psum", bufs=1))
+        transpose_psum = ctx.enter_context(tc.psum_pool(name="transpose_psum", bufs=2))
         score_psum = ctx.enter_context(tc.psum_pool(name="score_psum", bufs=SCORE_BANKS))
         out_psum = ctx.enter_context(tc.psum_pool(name="out_psum", bufs=2))
 
         q_sb, k_sb, v_sb = {}, {}, {}
+        qT_psum, kT_psum = {}, {}
         qT, kT, decay = {}, {}, {}
         v_grouped, v_codes, v_scales = {}, {}, {}
 
@@ -108,42 +114,31 @@ def tile_gatedmultiscaleretentionlayer_pb_kernel(tc, q_rot, k_rot, v, out):
         nc.vector.memset(grouped[0][:], 0.0)
         nc.vector.memset(grouped[2][:], 0.0)
 
-        def transposed(rows_sb, tag):
+        def transpose_rows(rows_sb):
             bank = transpose_psum.tile([P, TILES, P], BF16, tag="transposes")
             for n in range(TILES):
                 nc.tensor.transpose(bank[:, n, :], rows_sb[:, n, :], identity[:])
+            return bank
+
+        def to_sbuf(bank, tag):
             result = per_head.tile([P, TILES, P], BF16, tag=tag)
             nc.scalar.copy(out=result[:], in_=bank[:])
             return result
 
-        def prepare(h, part):
-            if part == 0:
-                kT[h] = transposed(k_sb.pop(h), "kT")
-                decay[h] = per_head.tile([P, P, TABLE_PLANES], F32, name="decay", tag="decay")
-                nc.scalar.activation(
-                    out=decay[h][:],
-                    in_=exponent[:],
-                    func=mybir.ActivationFunctionType.Exp,
-                    scale=math.log(1.0 - 2.0 ** (-5 - h)),
-                )
-            if part == 1:
-                qT[h] = transposed(q_sb.pop(h), "qT")
-            if part == 2:
-                v_grouped[h] = per_head.tile(
-                    [P, PASSES, FEAT, PACK], BF16, name="v_grouped", tag="v_grouped", align_bytes=64
-                )
-                nc.scalar.copy(
-                    out=v_grouped[h][:], in_=v_sb.pop(h)[:].rearrange("p (g t) d -> p g d t", t=PACK)
-                )
-
-        def quantise_v(h):
-            v_codes[h] = v_mx.tile([P, PASSES, FEAT], U32, name="v_codes", tag="v_codes", align_bytes=64)
-            v_scales[h] = v_mx.tile([P, PASSES, FEAT], U8, name="v_scales", tag="v_scales", align_bytes=64)
-            nc.vector.quantize_mx(
-                out=v_codes[h][:].rearrange("p g d -> p (g d)").bitcast(FP8X4),
-                scales=v_scales[h][:].rearrange("p g d -> p (g d)"),
-                in_=v_grouped.pop(h)[:].rearrange("p g d t -> p (g d t)"),
+        def make_decay(h):
+            decay[h] = per_head.tile([P, P, TABLE_PLANES], F32, name="decay", tag="decay")
+            nc.scalar.activation(
+                out=decay[h][:],
+                in_=exponent[:],
+                func=mybir.ActivationFunctionType.Exp,
+                scale=math.log(1.0 - 2.0 ** (-5 - h)),
             )
+
+        def regroup_v(h):
+            v_grouped[h] = per_head.tile(
+                [P, PASSES, FEAT, PACK], BF16, name="v_grouped", tag="v_grouped", align_bytes=64
+            )
+            nc.scalar.copy(out=v_grouped[h][:], in_=v_sb.pop(h)[:].rearrange("p (g t) d -> p g d t", t=PACK))
 
         def score_matmuls(h, r, c):
             g, first_query_tile = ROUNDS[r]
@@ -165,25 +160,23 @@ def tile_gatedmultiscaleretentionlayer_pb_kernel(tc, q_rot, k_rot, v, out):
             gamma = 1.0 - 2.0 ** (-5 - h)
             return gamma ** (P * (behind - PACK)), decay[h][:, :, 0:PACK]
 
-        def decay_on_vector(h, r, c, bank):
+        def multiply_by_decay(h, r, c, bank):
             planes = planes_of(r, c)
             factor, table = decay_of(h, r, c)
-            nc.vector.scalar_tensor_tensor(
-                out=grouped[r][:, c, :, 0:planes],
-                in0=bank[:, :, 0:planes],
-                scalar=factor,
-                in1=table,
-                op0=MULT,
-                op1=MULT,
-            )
-
-        def decay_on_gpsimd(h, r, c, bank):
-            planes = planes_of(r, c)
-            factor, table = decay_of(h, r, c)
-            staged = staging.tile([P, P * PACK], F32, tag="staged")
-            packed = staged[:, 0 : P * planes].rearrange("p (i t) -> p i t", t=planes)
-            nc.scalar.mul(out=packed, in_=bank[:, :, 0:planes], mul=factor)
-            nc.gpsimd.tensor_tensor(out=grouped[r][:, c, :, 0:planes], in0=packed, in1=table, op=MULT)
+            if on_gpsimd(r, c):
+                staged = staging.tile([P, P * PACK], F32, tag="staged")
+                packed = staged[:, 0 : P * planes].rearrange("p (i t) -> p i t", t=planes)
+                nc.scalar.mul(out=packed, in_=bank[:, :, 0:planes], mul=factor)
+                nc.gpsimd.tensor_tensor(out=grouped[r][:, c, :, 0:planes], in0=packed, in1=table, op=MULT)
+            else:
+                nc.vector.scalar_tensor_tensor(
+                    out=grouped[r][:, c, :, 0:planes],
+                    in0=bank[:, :, 0:planes],
+                    scalar=factor,
+                    in1=table,
+                    op0=MULT,
+                    op1=MULT,
+                )
 
         def quantise_scores(r):
             nc.vector.quantize_mx(
@@ -192,54 +185,70 @@ def tile_gatedmultiscaleretentionlayer_pb_kernel(tc, q_rot, k_rot, v, out):
                 in_=grouped[r][:].rearrange("p c i t -> p (c i t)"),
             )
 
-        def retention(h, half):
-            rounds_of_half = ((0,), (1, 2))[half]
-            bank = out_psum.tile([P, PACK, FEAT], F32, tag="out")
-            for c in range(PACK):
-                for r in rounds_of_half:
-                    g = ROUNDS[r][0]
-                    nc.tensor.matmul_mx(
-                        out=bank[:, c, :],
-                        lhsT=codes[r][:, c, :].bitcast(FP8X4),
-                        lhsT_scale=scales[r][:, c, :],
-                        rhs=v_codes[h][:, g, :].bitcast(FP8X4),
-                        rhs_scale=v_scales[h][:, g, :],
-                        start=(r == rounds_of_half[0]),
-                        stop=(r == rounds_of_half[-1]),
-                    )
-            result = stores.tile([P, PACK, FEAT], F32, tag="result")
-            nc.scalar.copy(out=result[:], in_=bank[:])
-            first = TILES * h + PACK * half
-            nc.sync.dma_start(out=out_rows[:, first : first + PACK, :], in_=result[:])
+        def quantise_v(h):
+            v_codes[h] = per_head.tile([P, PASSES, FEAT], U32, name="v_codes", tag="v_codes", align_bytes=64)
+            v_scales[h] = per_head.tile([P, PASSES, FEAT], U8, name="v_scales", tag="v_scales", align_bytes=64)
+            nc.vector.quantize_mx(
+                out=v_codes[h][:].rearrange("p g d -> p (g d)").bitcast(FP8X4),
+                scales=v_scales[h][:].rearrange("p g d -> p (g d)"),
+                in_=v_grouped.pop(h)[:].rearrange("p g d t -> p (g d t)"),
+            )
 
-        def retention_after(h, r):
-            if r == 0:
-                retention(h, 0)
-            if r == 2:
-                retention(h, 1)
+        def quantise(h):
+            quantise_scores(1)
+            quantise_v(h)
+            quantise_scores(2)
+            quantise_scores(0)
 
-        for part in range(3):
-            prepare(0, part)
+        def retention(h):
+            for half, rounds_of_half in enumerate(((0,), (1, 2))):
+                bank = out_psum.tile([P, PACK, FEAT], F32, tag="out")
+                for c in range(PACK):
+                    for r in rounds_of_half:
+                        g = ROUNDS[r][0]
+                        nc.tensor.matmul_mx(
+                            out=bank[:, c, :],
+                            lhsT=codes[r][:, c, :].bitcast(FP8X4),
+                            lhsT_scale=scales[r][:, c, :],
+                            rhs=v_codes[h][:, g, :].bitcast(FP8X4),
+                            rhs_scale=v_scales[h][:, g, :],
+                            start=(r == rounds_of_half[0]),
+                            stop=(r == rounds_of_half[-1]),
+                        )
+                result = stores.tile([P, PACK, FEAT], F32, tag="result")
+                nc.scalar.copy(out=result[:], in_=bank[:])
+                first = TILES * h + PACK * half
+                nc.sync.dma_start(out=out_rows[:, first : first + PACK, :], in_=result[:])
 
-        steps = [(h, r) for h in range(HEADS) for r in range(len(ROUNDS))]
-        for s, (h, r) in enumerate(steps):
-            if r == 0 and h + LOAD_AHEAD < HEADS:
+        kT[0] = to_sbuf(transpose_rows(k_sb.pop(0)), "kT")
+        qT[0] = to_sbuf(transpose_rows(q_sb.pop(0)), "qT")
+        make_decay(0)
+        work = [(h, r, c) for h in range(HEADS) for (r, c) in BANKS]
+        filled = {}
+        for item in work[0:SCORE_BANKS]:
+            filled[item] = score_matmuls(*item)
+        for place, (h, r, c) in enumerate(work):
+            place_in_head = place % len(BANKS)
+            more_heads = h + 1 < HEADS
+            if place_in_head == 0 and h + LOAD_AHEAD < HEADS:
                 load(h + LOAD_AHEAD)
-            banks = [score_matmuls(h, r, c) for c in range(PACK)]
-            for c in range(PACK):
-                if on_gpsimd(r, c):
-                    decay_on_gpsimd(h, r, c, banks[c])
-            if h + 1 < HEADS:
-                prepare(h + 1, r)
-            if s >= 2:
-                retention_after(*steps[s - 2])
-            for c in range(PACK):
-                if not on_gpsimd(r, c):
-                    decay_on_vector(h, r, c, banks[c])
-            if s >= 1:
-                quantise_scores(steps[s - 1][1])
-            if r == 0:
-                quantise_v(h)
-        retention_after(*steps[-2])
-        quantise_scores(steps[-1][1])
-        retention_after(*steps[-1])
+            if place_in_head == 1 and more_heads:
+                kT_psum[h + 1] = transpose_rows(k_sb.pop(h + 1))
+            if place_in_head == 2 and more_heads:
+                qT_psum[h + 1] = transpose_rows(q_sb.pop(h + 1))
+            if place_in_head == len(GPSIMD_BANKS):
+                if more_heads:
+                    kT[h + 1] = to_sbuf(kT_psum.pop(h + 1), "kT")
+                    qT[h + 1] = to_sbuf(qT_psum.pop(h + 1), "qT")
+                regroup_v(h)
+                if more_heads:
+                    make_decay(h + 1)
+                if h > 0:
+                    retention(h - 1)
+            multiply_by_decay(h, r, c, filled.pop((h, r, c)))
+            if place + SCORE_BANKS < len(work):
+                ahead = work[place + SCORE_BANKS]
+                filled[ahead] = score_matmuls(*ahead)
+            if place_in_head == len(BANKS) - 1:
+                quantise(h)
+        retention(HEADS - 1)

@@ -25,7 +25,6 @@ ROUNDS = ((0, 0), (0, 4), (1, 4))
 TABLE_PLANES = PACK + 1
 
 GPSIMD_MAX_PLANES = 2
-GPSIMD_FULL_BANKS = 1
 
 LOAD_AHEAD = 3
 SCORE_BANKS = 4
@@ -43,7 +42,7 @@ def planes_of(r, c):
 
 
 def on_gpsimd(r, c):
-    return planes_of(r, c) <= GPSIMD_MAX_PLANES or (r == 1 and c < GPSIMD_FULL_BANKS)
+    return planes_of(r, c) <= GPSIMD_MAX_PLANES or (r == 0 and planes_of(r, c) < PACK)
 
 
 ALL_BANKS = [(r, c) for r in range(len(ROUNDS)) for c in range(PACK)]
@@ -201,7 +200,7 @@ def tile_gatedmultiscaleretentionlayer_pb_kernel(tc, q_rot, k_rot, v, out):
             quantise_scores(0)
 
         def retention(h):
-            for half, rounds_of_half in enumerate(((0,), (1, 2))):
+            for half, rounds_of_half in ((1, (1, 2)), (0, (0,))):
                 bank = out_psum.tile([P, PACK, FEAT], F32, tag="out")
                 for c in range(PACK):
                     for r in rounds_of_half:
@@ -220,9 +219,9 @@ def tile_gatedmultiscaleretentionlayer_pb_kernel(tc, q_rot, k_rot, v, out):
                 first = TILES * h + PACK * half
                 nc.sync.dma_start(out=out_rows[:, first : first + PACK, :], in_=result[:])
 
+        make_decay(0)
         kT[0] = to_sbuf(transpose_rows(k_sb.pop(0)), "kT")
         qT[0] = to_sbuf(transpose_rows(q_sb.pop(0)), "qT")
-        make_decay(0)
         work = [(h, r, c) for h in range(HEADS) for (r, c) in BANKS]
         filled = {}
         for item in work[0:SCORE_BANKS]:

@@ -141,10 +141,10 @@ def tile_gatedmultiscaleretentionlayer_pb_kernel(tc, q_rot, k_rot, v, out):
 
         def score_matmuls(h, r, c):
             g, first_query_tile = ROUNDS[r]
-            bank = score_psum.tile([P, P, PACK], F32, tag="scores")
+            bank = score_psum.tile([P, PACK, P], F32, tag="scores")
             for t in range(planes_of(r, c)):
                 nc.tensor.matmul(
-                    out=bank[:, :, t],
+                    out=bank[:, t, :],
                     lhsT=kT[h][:, PACK * g + t, :],
                     rhs=qT[h][:, first_query_tile + c, :],
                     start=True,
@@ -162,15 +162,16 @@ def tile_gatedmultiscaleretentionlayer_pb_kernel(tc, q_rot, k_rot, v, out):
         def multiply_by_decay(h, r, c, bank):
             planes = planes_of(r, c)
             factor, table = decay_of(h, r, c)
+            interleaved = bank[:, 0:planes, :].rearrange("p t i -> p i t")
             if on_gpsimd(r, c):
                 staged = staging.tile([P, P * PACK], F32, tag="staged")
                 packed = staged[:, 0 : P * planes].rearrange("p (i t) -> p i t", t=planes)
-                nc.scalar.mul(out=packed, in_=bank[:, :, 0:planes], mul=factor)
+                nc.scalar.mul(out=packed, in_=interleaved, mul=factor)
                 nc.gpsimd.tensor_tensor(out=grouped[r][:, c, :, 0:planes], in0=packed, in1=table, op=MULT)
             else:
                 nc.vector.scalar_tensor_tensor(
                     out=grouped[r][:, c, :, 0:planes],
-                    in0=bank[:, :, 0:planes],
+                    in0=interleaved,
                     scalar=factor,
                     in1=table,
                     op0=MULT,

@@ -24,8 +24,6 @@ ROUNDS = ((0, 0), (0, 4), (1, 4))
 
 TABLE_PLANES = PACK + 1
 
-GPSIMD_MAX_PLANES = 2
-
 LOAD_AHEAD = 3
 SCORE_BANKS = 4
 
@@ -41,13 +39,10 @@ def planes_of(r, c):
     return min(tiles_behind(r, c) + 1, PACK)
 
 
-def on_gpsimd(r, c):
-    return planes_of(r, c) <= GPSIMD_MAX_PLANES or (r == 0 and planes_of(r, c) < PACK)
+SLOT = {1: 0, 0: 1, 2: 2}
 
-
-ALL_BANKS = [(r, c) for r in range(len(ROUNDS)) for c in range(PACK)]
-GPSIMD_BANKS = [rc for rc in ALL_BANKS if on_gpsimd(*rc)]
-VECTOR_BANKS = [rc for rc in ALL_BANKS if not on_gpsimd(*rc)]
+GPSIMD_BANKS = [((0, 2), 0), ((0, 2), 1), ((0,), 2)]
+VECTOR_BANKS = [((1,), 0), ((1,), 1), ((1,), 2), ((1,), 3), ((2,), 2), ((0,), 3), ((2,), 3)]
 BANKS = GPSIMD_BANKS + VECTOR_BANKS
 
 
@@ -103,15 +98,10 @@ def tile_gatedmultiscaleretentionlayer_pb_kernel(tc, q_rot, k_rot, v, out):
             op1=mybir.AluOpType.max,
         )
 
-        grouped = []
-        codes = []
-        scales = []
-        for r in range(len(ROUNDS)):
-            grouped.append(fixed.tile([P, PACK, P, PACK], BF16, name="grouped%d" % r, align_bytes=64))
-            codes.append(fixed.tile([P, PACK, P], U32, name="codes%d" % r, align_bytes=64))
-            scales.append(fixed.tile([P, PACK, P], U8, name="scales%d" % r, align_bytes=64))
-        nc.vector.memset(grouped[0][:], 0.0)
-        nc.vector.memset(grouped[2][:], 0.0)
+        grouped = fixed.tile([P, len(ROUNDS), PACK, P, PACK], BF16, name="grouped", align_bytes=64)
+        codes = fixed.tile([P, len(ROUNDS), PACK, P], U32, name="codes", align_bytes=64)
+        scales = fixed.tile([P, len(ROUNDS), PACK, P], U8, name="scales", align_bytes=64)
+        nc.vector.memset(grouped[:, SLOT[0] : SLOT[2] + 1, :, :, :].rearrange("p s c i t -> p (s c i t)"), 0.0)
 
         def transpose_rows(rows_sb):
             bank = transpose_psum.tile([P, TILES, P], BF16, tag="transposes")
@@ -139,17 +129,20 @@ def tile_gatedmultiscaleretentionlayer_pb_kernel(tc, q_rot, k_rot, v, out):
             )
             nc.scalar.copy(out=v_grouped[h][:], in_=v_sb.pop(h)[:].rearrange("p (g t) d -> p g d t", t=PACK))
 
-        def score_matmuls(h, r, c):
-            g, first_query_tile = ROUNDS[r]
+        def score_matmuls(h, rounds, c):
             bank = score_psum.tile([P, PACK, P], F32, tag="scores")
-            for t in range(planes_of(r, c)):
-                nc.tensor.matmul(
-                    out=bank[:, t, :],
-                    lhsT=kT[h][:, PACK * g + t, :],
-                    rhs=qT[h][:, first_query_tile + c, :],
-                    start=True,
-                    stop=True,
-                )
+            n = 0
+            for r in rounds:
+                g, first_query_tile = ROUNDS[r]
+                for t in range(planes_of(r, c)):
+                    nc.tensor.matmul(
+                        out=bank[:, n, :],
+                        lhsT=kT[h][:, PACK * g + t, :],
+                        rhs=qT[h][:, first_query_tile + c, :],
+                        start=True,
+                        stop=True,
+                    )
+                    n += 1
             return bank
 
         def decay_of(h, r, c):
@@ -159,30 +152,39 @@ def tile_gatedmultiscaleretentionlayer_pb_kernel(tc, q_rot, k_rot, v, out):
             gamma = 1.0 - 2.0 ** (-5 - h)
             return gamma ** (P * (behind - PACK)), decay[h][:, :, 0:PACK]
 
-        def multiply_by_decay(h, r, c, bank):
+        def multiply_by_decay(h, rounds, c, bank):
+            r = rounds[0]
             planes = planes_of(r, c)
             factor, table = decay_of(h, r, c)
-            interleaved = bank[:, 0:planes, :].rearrange("p t i -> p i t")
-            if on_gpsimd(r, c):
+            if (rounds, c) in GPSIMD_BANKS:
+                count = len(rounds)
                 staged = staging.tile([P, P * PACK], F32, tag="staged")
-                packed = staged[:, 0 : P * planes].rearrange("p (i t) -> p i t", t=planes)
-                nc.scalar.mul(out=packed, in_=interleaved, mul=factor)
-                nc.gpsimd.tensor_tensor(out=grouped[r][:, c, :, 0:planes], in0=packed, in1=table, op=MULT)
+                packed = staged[:, 0 : count * P * planes].rearrange("p (r i t) -> p r i t", r=count, t=planes)
+                nc.scalar.copy(
+                    out=packed, in_=bank[:, 0 : count * planes, :].rearrange("p (r t) i -> p r i t", r=count)
+                )
+                nc.gpsimd.tensor_tensor(
+                    out=grouped[:, SLOT[r] : SLOT[r] + count, c, :, 0:planes],
+                    in0=packed,
+                    in1=table.unsqueeze(1).to_broadcast([P, count, P, planes]),
+                    op=MULT,
+                )
             else:
                 nc.vector.scalar_tensor_tensor(
-                    out=grouped[r][:, c, :, 0:planes],
-                    in0=interleaved,
+                    out=grouped[:, SLOT[r], c, :, 0:planes],
+                    in0=bank[:, 0:planes, :].rearrange("p t i -> p i t"),
                     scalar=factor,
                     in1=table,
                     op0=MULT,
                     op1=MULT,
                 )
 
-        def quantise_scores(r):
+        def quantise_scores(first_slot, slots):
+            these = slice(first_slot, first_slot + slots)
             nc.vector.quantize_mx(
-                out=codes[r][:].rearrange("p c i -> p (c i)").bitcast(FP8X4),
-                scales=scales[r][:].rearrange("p c i -> p (c i)"),
-                in_=grouped[r][:].rearrange("p c i t -> p (c i t)"),
+                out=codes[:, these, :, :].rearrange("p s c i -> p (s c i)").bitcast(FP8X4),
+                scales=scales[:, these, :, :].rearrange("p s c i -> p (s c i)"),
+                in_=grouped[:, these, :, :, :].rearrange("p s c i t -> p (s c i t)"),
             )
 
         def quantise_v(h):
@@ -195,10 +197,9 @@ def tile_gatedmultiscaleretentionlayer_pb_kernel(tc, q_rot, k_rot, v, out):
             )
 
         def quantise(h):
-            quantise_scores(1)
+            quantise_scores(SLOT[1], 1)
             quantise_v(h)
-            quantise_scores(2)
-            quantise_scores(0)
+            quantise_scores(SLOT[0], 2)
 
         def retention(h):
             for half, rounds_of_half in ((1, (1, 2)), (0, (0,))):
@@ -208,8 +209,8 @@ def tile_gatedmultiscaleretentionlayer_pb_kernel(tc, q_rot, k_rot, v, out):
                         g = ROUNDS[r][0]
                         nc.tensor.matmul_mx(
                             out=bank[:, c, :],
-                            lhsT=codes[r][:, c, :].bitcast(FP8X4),
-                            lhsT_scale=scales[r][:, c, :],
+                            lhsT=codes[:, SLOT[r], c, :].bitcast(FP8X4),
+                            lhsT_scale=scales[:, SLOT[r], c, :],
                             rhs=v_codes[h][:, g, :].bitcast(FP8X4),
                             rhs_scale=v_scales[h][:, g, :],
                             start=(r == rounds_of_half[0]),
@@ -223,11 +224,11 @@ def tile_gatedmultiscaleretentionlayer_pb_kernel(tc, q_rot, k_rot, v, out):
         make_decay(0)
         kT[0] = to_sbuf(transpose_rows(k_sb.pop(0)), "kT")
         qT[0] = to_sbuf(transpose_rows(q_sb.pop(0)), "qT")
-        work = [(h, r, c) for h in range(HEADS) for (r, c) in BANKS]
+        work = [(h, rounds, c) for h in range(HEADS) for (rounds, c) in BANKS]
         filled = {}
         for item in work[0:SCORE_BANKS]:
             filled[item] = score_matmuls(*item)
-        for place, (h, r, c) in enumerate(work):
+        for place, (h, rounds, c) in enumerate(work):
             place_in_head = place % len(BANKS)
             more_heads = h + 1 < HEADS
             if place_in_head == 0 and h + LOAD_AHEAD < HEADS:
@@ -245,7 +246,7 @@ def tile_gatedmultiscaleretentionlayer_pb_kernel(tc, q_rot, k_rot, v, out):
                     make_decay(h + 1)
                 if h > 0:
                     retention(h - 1)
-            multiply_by_decay(h, r, c, filled.pop((h, r, c)))
+            multiply_by_decay(h, rounds, c, filled.pop((h, rounds, c)))
             if place + SCORE_BANKS < len(work):
                 ahead = work[place + SCORE_BANKS]
                 filled[ahead] = score_matmuls(*ahead)

@@ -59,7 +59,7 @@ def tile_gatedmultiscaleretentionlayer_pb_kernel(tc, q_rot, k_rot, v, out):
         loads = ctx.enter_context(tc.tile_pool(name="loads", bufs=LOAD_AHEAD + 1))
         per_head = ctx.enter_context(tc.tile_pool(name="per_head", bufs=2))
         staging = ctx.enter_context(tc.tile_pool(name="staging", bufs=len(GPSIMD_BANKS)))
-        stores = ctx.enter_context(tc.tile_pool(name="stores", bufs=4))
+        stores = ctx.enter_context(tc.tile_pool(name="stores", bufs=6))
         transpose_psum = ctx.enter_context(tc.psum_pool(name="transpose_psum", bufs=2))
         score_psum = ctx.enter_context(tc.psum_pool(name="score_psum", bufs=SCORE_BANKS))
         out_psum = ctx.enter_context(tc.psum_pool(name="out_psum", bufs=2))
@@ -81,13 +81,19 @@ def tile_gatedmultiscaleretentionlayer_pb_kernel(tc, q_rot, k_rot, v, out):
         for h in range(LOAD_AHEAD):
             load(h)
 
-        identity = fixed.tile([P, P], BF16)
-        make_identity(nc, identity[:])
+        grouped = fixed.tile([P, len(ROUNDS), PACK, P, PACK], BF16, name="grouped", align_bytes=64)
+        codes = fixed.tile([P, len(ROUNDS), PACK, P], U32, name="codes", align_bytes=64)
+        scales = fixed.tile([P, len(ROUNDS), PACK, P], U8, name="scales", align_bytes=64)
+        nc.vector.memset(
+            grouped[:, SLOT[0] : SLOT[2] + 1, 0 : PACK - 1, :, :].rearrange("p s c i t -> p s (c i t)").bitcast(I32), 0
+        )
 
         distance = fixed.tile([P, P, TABLE_PLANES], I32)
         nc.gpsimd.iota(
             distance[:], pattern=[[1, P], [-P, TABLE_PLANES]], base=P * PACK, channel_multiplier=-1
         )
+        identity = fixed.tile([P, P], BF16)
+        make_identity(nc, identity[:])
         exponent = fixed.tile([P, P, TABLE_PLANES], F32)
         nc.vector.scalar_tensor_tensor(
             out=exponent[:],
@@ -98,10 +104,6 @@ def tile_gatedmultiscaleretentionlayer_pb_kernel(tc, q_rot, k_rot, v, out):
             op1=mybir.AluOpType.max,
         )
 
-        grouped = fixed.tile([P, len(ROUNDS), PACK, P, PACK], BF16, name="grouped", align_bytes=64)
-        codes = fixed.tile([P, len(ROUNDS), PACK, P], U32, name="codes", align_bytes=64)
-        scales = fixed.tile([P, len(ROUNDS), PACK, P], U8, name="scales", align_bytes=64)
-        nc.vector.memset(grouped[:, SLOT[0] : SLOT[2] + 1, :, :, :].rearrange("p s c i t -> p (s c i t)"), 0.0)
 
         def transpose_rows(rows_sb):
             bank = transpose_psum.tile([P, TILES, P], BF16, tag="transposes")
@@ -201,25 +203,56 @@ def tile_gatedmultiscaleretentionlayer_pb_kernel(tc, q_rot, k_rot, v, out):
             quantise_v(h)
             quantise_scores(SLOT[0], 2)
 
+        def mx_pass(acc, h, r, c, start, stop):
+            g = ROUNDS[r][0]
+            nc.tensor.matmul_mx(
+                out=acc,
+                lhsT=codes[:, SLOT[r], c, :].bitcast(FP8X4),
+                lhsT_scale=scales[:, SLOT[r], c, :],
+                rhs=v_codes[h][:, g, :].bitcast(FP8X4),
+                rhs_scale=v_scales[h][:, g, :],
+                start=start,
+                stop=stop,
+            )
+
+        def store(h, first_tile, result):
+            first = TILES * h + first_tile
+            nc.sync.dma_start(out=out_rows[:, first : first + result.shape[1], :], in_=result)
+
         def retention(h):
             for half, rounds_of_half in ((1, (1, 2)), (0, (0,))):
                 bank = out_psum.tile([P, PACK, FEAT], F32, tag="out")
                 for c in range(PACK):
                     for r in rounds_of_half:
-                        g = ROUNDS[r][0]
-                        nc.tensor.matmul_mx(
-                            out=bank[:, c, :],
-                            lhsT=codes[:, SLOT[r], c, :].bitcast(FP8X4),
-                            lhsT_scale=scales[:, SLOT[r], c, :],
-                            rhs=v_codes[h][:, g, :].bitcast(FP8X4),
-                            rhs_scale=v_scales[h][:, g, :],
-                            start=(r == rounds_of_half[0]),
-                            stop=(r == rounds_of_half[-1]),
-                        )
+                        mx_pass(bank[:, c, :], h, r, c, r == rounds_of_half[0], r == rounds_of_half[-1])
                 result = stores.tile([P, PACK, FEAT], F32, tag="result")
                 nc.scalar.copy(out=result[:], in_=bank[:])
-                first = TILES * h + PACK * half
-                nc.sync.dma_start(out=out_rows[:, first : first + PACK, :], in_=result[:])
+                store(h, PACK * half, result[:])
+
+        def finish(h):
+            quantise_v(h)
+            quantise_scores(SLOT[0], 1)
+            bank = out_psum.tile([P, PACK, FEAT], F32, tag="out")
+            for c in range(PACK):
+                mx_pass(bank[:, c, :], h, 0, c, True, True)
+            for first_tile in (0, 2):
+                result = stores.tile([P, PACK, FEAT], F32, tag="result")
+                nc.scalar.copy(out=result[:, 0:2, :], in_=bank[:, first_tile : first_tile + 2, :])
+                store(h, first_tile, result[:, 0:2, :])
+            quantise_scores(SLOT[1], 1)
+            banks = []
+            for c in range(PACK):
+                banks.append(score_psum.tile([P, PACK, FEAT], F32, name="last", tag="scores"))
+                mx_pass(banks[c][:, 0, :], h, 1, c, True, False)
+            quantise_scores(SLOT[2], 1)
+            for c in range(PACK):
+                mx_pass(banks[c][:, 0, :], h, 2, c, False, True)
+                result = stores.tile([P, PACK, FEAT], F32, tag="result")
+                if c % 2 == 0:
+                    nc.vector.tensor_copy(out=result[:, 0:1, :], in_=banks[c][:, 0:1, :])
+                else:
+                    nc.scalar.copy(out=result[:, 0:1, :], in_=banks[c][:, 0:1, :])
+                store(h, PACK + c, result[:, 0:1, :])
 
         make_decay(0)
         kT[0] = to_sbuf(transpose_rows(k_sb.pop(0)), "kT")
@@ -251,5 +284,7 @@ def tile_gatedmultiscaleretentionlayer_pb_kernel(tc, q_rot, k_rot, v, out):
                 ahead = work[place + SCORE_BANKS]
                 filled[ahead] = score_matmuls(*ahead)
             if place_in_head == len(BANKS) - 1:
-                quantise(h)
-        retention(HEADS - 1)
+                if more_heads:
+                    quantise(h)
+                else:
+                    finish(h)

import math
from contextlib import ExitStack

import concourse.mybir as mybir
from concourse.masks import make_identity

BF16 = mybir.dt.bfloat16
F32 = mybir.dt.float32
I32 = mybir.dt.int32
U32 = mybir.dt.uint32
U8 = mybir.dt.uint8
FP8X4 = mybir.dt.float8_e4m3fn_x4
MULT = mybir.AluOpType.mult

HEADS = 16
SEQ = 1024
FEAT = 128
P = 128
PACK = 4
TILES = SEQ // P
PASSES = SEQ // (P * PACK)

ROUNDS = ((0, 0), (0, 4), (1, 4))

TABLE_PLANES = PACK + 1

LOAD_AHEAD = 3
SCORE_BANKS = 4

FLOPS = 2 * 2 * HEADS * FEAT * (512 * 512 + 512 * 1024)


def tiles_behind(r, c):
    g, first_query_tile = ROUNDS[r]
    return first_query_tile + c - PACK * g


def planes_of(r, c):
    return min(tiles_behind(r, c) + 1, PACK)


SLOT = {1: 0, 0: 1, 2: 2}

GPSIMD_BANKS = [((0, 2), 0), ((0, 2), 1), ((0,), 2)]
VECTOR_BANKS = [((1,), 0), ((1,), 1), ((1,), 2), ((1,), 3), ((2,), 2), ((0,), 3), ((2,), 3)]
BANKS = GPSIMD_BANKS + VECTOR_BANKS


def tile_gatedmultiscaleretentionlayer_pb_kernel(tc, q_rot, k_rot, v, out):
    nc = tc.nc
    q_rows = q_rot.rearrange("b h (n p) d -> p (b h n) d", p=P)
    k_rows = k_rot.rearrange("b h (n p) d -> p (b h n) d", p=P)
    v_rows = v.rearrange("b h (n p) d -> p (b h n) d", p=P)
    out_rows = out.rearrange("b h (n p) d -> p (b h n) d", p=P)

    with ExitStack() as ctx:
        ctx.enter_context(tc.manual_schedule())
        fixed = ctx.enter_context(tc.tile_pool(name="fixed", bufs=1))
        loads = ctx.enter_context(tc.tile_pool(name="loads", bufs=LOAD_AHEAD + 1))
        per_head = ctx.enter_context(tc.tile_pool(name="per_head", bufs=2))
        staging = ctx.enter_context(tc.tile_pool(name="staging", bufs=len(GPSIMD_BANKS)))
        stores = ctx.enter_context(tc.tile_pool(name="stores", bufs=6))
        transpose_psum = ctx.enter_context(tc.psum_pool(name="transpose_psum", bufs=2))
        score_psum = ctx.enter_context(tc.psum_pool(name="score_psum", bufs=SCORE_BANKS))
        out_psum = ctx.enter_context(tc.psum_pool(name="out_psum", bufs=2))

        q_sb, k_sb, v_sb = {}, {}, {}
        qT_psum, kT_psum = {}, {}
        qT, kT, decay = {}, {}, {}
        v_grouped, v_codes, v_scales = {}, {}, {}

        def load(h):
            rows = slice(TILES * h, TILES * (h + 1))
            k_sb[h] = loads.tile([P, TILES, FEAT], BF16, name="k_sb", tag="k_sb")
            nc.sync.dma_start(out=k_sb[h][:], in_=k_rows[:, rows, :])
            q_sb[h] = loads.tile([P, TILES, FEAT], BF16, name="q_sb", tag="q_sb")
            nc.sync.dma_start(out=q_sb[h][:], in_=q_rows[:, rows, :])
            v_sb[h] = loads.tile([P, TILES, FEAT], BF16, name="v_sb", tag="v_sb")
            nc.sync.dma_start(out=v_sb[h][:], in_=v_rows[:, rows, :])

        for h in range(LOAD_AHEAD):
            load(h)

        grouped = fixed.tile([P, len(ROUNDS), PACK, P, PACK], BF16, name="grouped", align_bytes=64)
        codes = fixed.tile([P, len(ROUNDS), PACK, P], U32, name="codes", align_bytes=64)
        scales = fixed.tile([P, len(ROUNDS), PACK, P], U8, name="scales", align_bytes=64)
        nc.vector.memset(
            grouped[:, SLOT[0] : SLOT[2] + 1, 0 : PACK - 1, :, :].rearrange("p s c i t -> p s (c i t)").bitcast(I32), 0
        )

        distance = fixed.tile([P, P, TABLE_PLANES], I32)
        nc.gpsimd.iota(
            distance[:], pattern=[[1, P], [-P, TABLE_PLANES]], base=P * PACK, channel_multiplier=-1
        )
        identity = fixed.tile([P, P], BF16)
        make_identity(nc, identity[:])
        exponent = fixed.tile([P, P, TABLE_PLANES], F32)
        nc.vector.scalar_tensor_tensor(
            out=exponent[:],
            in0=distance[:],
            scalar=-(2.0**30),
            in1=distance[:],
            op0=MULT,
            op1=mybir.AluOpType.max,
        )


        def transpose_rows(rows_sb):
            bank = transpose_psum.tile([P, TILES, P], BF16, tag="transposes")
            for n in range(TILES):
                nc.tensor.transpose(bank[:, n, :], rows_sb[:, n, :], identity[:])
            return bank

        def to_sbuf(bank, tag):
            result = per_head.tile([P, TILES, P], BF16, tag=tag)
            nc.scalar.copy(out=result[:], in_=bank[:])
            return result

        def make_decay(h):
            decay[h] = per_head.tile([P, P, TABLE_PLANES], F32, name="decay", tag="decay")
            nc.scalar.activation(
                out=decay[h][:],
                in_=exponent[:],
                func=mybir.ActivationFunctionType.Exp,
                scale=math.log(1.0 - 2.0 ** (-5 - h)),
            )

        def regroup_v(h):
            v_grouped[h] = per_head.tile(
                [P, PASSES, FEAT, PACK], BF16, name="v_grouped", tag="v_grouped", align_bytes=64
            )
            nc.scalar.copy(out=v_grouped[h][:], in_=v_sb.pop(h)[:].rearrange("p (g t) d -> p g d t", t=PACK))

        def score_matmuls(h, rounds, c):
            bank = score_psum.tile([P, PACK, P], F32, tag="scores")
            n = 0
            for r in rounds:
                g, first_query_tile = ROUNDS[r]
                for t in range(planes_of(r, c)):
                    nc.tensor.matmul(
                        out=bank[:, n, :],
                        lhsT=kT[h][:, PACK * g + t, :],
                        rhs=qT[h][:, first_query_tile + c, :],
                        start=True,
                        stop=True,
                    )
                    n += 1
            return bank

        def decay_of(h, r, c):
            behind = tiles_behind(r, c)
            if behind < PACK:
                return 1.0, decay[h][:, :, PACK - behind : TABLE_PLANES]
            gamma = 1.0 - 2.0 ** (-5 - h)
            return gamma ** (P * (behind - PACK)), decay[h][:, :, 0:PACK]

        def multiply_by_decay(h, rounds, c, bank):
            r = rounds[0]
            planes = planes_of(r, c)
            factor, table = decay_of(h, r, c)
            if (rounds, c) in GPSIMD_BANKS:
                count = len(rounds)
                staged = staging.tile([P, P * PACK], F32, tag="staged")
                packed = staged[:, 0 : count * P * planes].rearrange("p (r i t) -> p r i t", r=count, t=planes)
                nc.scalar.copy(
                    out=packed, in_=bank[:, 0 : count * planes, :].rearrange("p (r t) i -> p r i t", r=count)
                )
                nc.gpsimd.tensor_tensor(
                    out=grouped[:, SLOT[r] : SLOT[r] + count, c, :, 0:planes],
                    in0=packed,
                    in1=table.unsqueeze(1).to_broadcast([P, count, P, planes]),
                    op=MULT,
                )
            else:
                nc.vector.scalar_tensor_tensor(
                    out=grouped[:, SLOT[r], c, :, 0:planes],
                    in0=bank[:, 0:planes, :].rearrange("p t i -> p i t"),
                    scalar=factor,
                    in1=table,
                    op0=MULT,
                    op1=MULT,
                )

        def quantise_scores(first_slot, slots):
            these = slice(first_slot, first_slot + slots)
            nc.vector.quantize_mx(
                out=codes[:, these, :, :].rearrange("p s c i -> p (s c i)").bitcast(FP8X4),
                scales=scales[:, these, :, :].rearrange("p s c i -> p (s c i)"),
                in_=grouped[:, these, :, :, :].rearrange("p s c i t -> p (s c i t)"),
            )

        def quantise_v(h):
            v_codes[h] = per_head.tile([P, PASSES, FEAT], U32, name="v_codes", tag="v_codes", align_bytes=64)
            v_scales[h] = per_head.tile([P, PASSES, FEAT], U8, name="v_scales", tag="v_scales", align_bytes=64)
            nc.vector.quantize_mx(
                out=v_codes[h][:].rearrange("p g d -> p (g d)").bitcast(FP8X4),
                scales=v_scales[h][:].rearrange("p g d -> p (g d)"),
                in_=v_grouped.pop(h)[:].rearrange("p g d t -> p (g d t)"),
            )

        def quantise(h):
            quantise_scores(SLOT[1], 1)
            quantise_v(h)
            quantise_scores(SLOT[0], 2)

        def mx_pass(acc, h, r, c, start, stop):
            g = ROUNDS[r][0]
            nc.tensor.matmul_mx(
                out=acc,
                lhsT=codes[:, SLOT[r], c, :].bitcast(FP8X4),
                lhsT_scale=scales[:, SLOT[r], c, :],
                rhs=v_codes[h][:, g, :].bitcast(FP8X4),
                rhs_scale=v_scales[h][:, g, :],
                start=start,
                stop=stop,
            )

        def store(h, first_tile, result):
            first = TILES * h + first_tile
            nc.sync.dma_start(out=out_rows[:, first : first + result.shape[1], :], in_=result)

        def retention(h):
            for half, rounds_of_half in ((1, (1, 2)), (0, (0,))):
                bank = out_psum.tile([P, PACK, FEAT], F32, tag="out")
                for c in range(PACK):
                    for r in rounds_of_half:
                        mx_pass(bank[:, c, :], h, r, c, r == rounds_of_half[0], r == rounds_of_half[-1])
                result = stores.tile([P, PACK, FEAT], F32, tag="result")
                nc.scalar.copy(out=result[:], in_=bank[:])
                store(h, PACK * half, result[:])

        def finish(h):
            quantise_v(h)
            quantise_scores(SLOT[0], 1)
            bank = out_psum.tile([P, PACK, FEAT], F32, tag="out")
            for c in range(PACK):
                mx_pass(bank[:, c, :], h, 0, c, True, True)
            for first_tile in (0, 2):
                result = stores.tile([P, PACK, FEAT], F32, tag="result")
                nc.scalar.copy(out=result[:, 0:2, :], in_=bank[:, first_tile : first_tile + 2, :])
                store(h, first_tile, result[:, 0:2, :])
            quantise_scores(SLOT[1], 1)
            banks = []
            for c in range(PACK):
                banks.append(score_psum.tile([P, PACK, FEAT], F32, name="last", tag="scores"))
                mx_pass(banks[c][:, 0, :], h, 1, c, True, False)
            quantise_scores(SLOT[2], 1)
            for c in range(PACK):
                mx_pass(banks[c][:, 0, :], h, 2, c, False, True)
                result = stores.tile([P, PACK, FEAT], F32, tag="result")
                if c % 2 == 0:
                    nc.vector.tensor_copy(out=result[:, 0:1, :], in_=banks[c][:, 0:1, :])
                else:
                    nc.scalar.copy(out=result[:, 0:1, :], in_=banks[c][:, 0:1, :])
                store(h, PACK + c, result[:, 0:1, :])

        make_decay(0)
        kT[0] = to_sbuf(transpose_rows(k_sb.pop(0)), "kT")
        qT[0] = to_sbuf(transpose_rows(q_sb.pop(0)), "qT")
        work = [(h, rounds, c) for h in range(HEADS) for (rounds, c) in BANKS]
        filled = {}
        for item in work[0:SCORE_BANKS]:
            filled[item] = score_matmuls(*item)
        for place, (h, rounds, c) in enumerate(work):
            place_in_head = place % len(BANKS)
            more_heads = h + 1 < HEADS
            if place_in_head == 0 and h + LOAD_AHEAD < HEADS:
                load(h + LOAD_AHEAD)
            if place_in_head == 1 and more_heads:
                kT_psum[h + 1] = transpose_rows(k_sb.pop(h + 1))
            if place_in_head == 2 and more_heads:
                qT_psum[h + 1] = transpose_rows(q_sb.pop(h + 1))
            if place_in_head == len(GPSIMD_BANKS):
                if more_heads:
                    kT[h + 1] = to_sbuf(kT_psum.pop(h + 1), "kT")
                    qT[h + 1] = to_sbuf(qT_psum.pop(h + 1), "qT")
                regroup_v(h)
                if more_heads:
                    make_decay(h + 1)
                if h > 0:
                    retention(h - 1)
            multiply_by_decay(h, rounds, c, filled.pop((h, rounds, c)))
            if place + SCORE_BANKS < len(work):
                ahead = work[place + SCORE_BANKS]
                filled[ahead] = score_matmuls(*ahead)
            if place_in_head == len(BANKS) - 1:
                if more_heads:
                    quantise(h)
                else:
                    finish(h)
